import numpy as np
import ml_dtypes


def mxq(x, axis, fmt="e4m3"):
    dtype, down = {"e4m3": (ml_dtypes.float8_e4m3fn, 7), "e5m2": (ml_dtypes.float8_e5m2, 14)}[fmt]
    v = np.moveaxis(np.asarray(x, np.float32).astype(ml_dtypes.bfloat16).astype(np.float64), axis, -1)
    blocks = v.reshape(v.shape[:-1] + (-1, 32))
    amax = np.abs(blocks).max(-1, keepdims=True)
    byte = np.maximum(np.where(amax > 0, np.frexp(amax)[1] - 1 + 127, 0) - down, 1)
    scale = np.exp2(byte - 127.0)
    codes = (blocks / scale).astype(np.float32).astype(dtype).astype(np.float64)
    return np.moveaxis((codes * scale).reshape(v.shape), -1, axis)


WIDE = False


def mx_kscale(k):
    if not WIDE:
        return np.ones(k)
    levels = np.array([10, -10, 5, -5, 0])
    a = np.random.permutation(np.resize(levels, k // 512 * 4)).reshape(k // 512, 4)
    idx = np.arange(k)
    return np.exp2(a[idx // 512, idx % 128 // 32])


BF16 = ml_dtypes.bfloat16


def bf(x):
    return np.asarray(x, np.float32).astype(BF16)


def f64(x):
    return np.asarray(x).astype(np.float64)


E2M1 = np.array([0.0, 0.5, 1.0, 1.5, 2.0, 3.0, 4.0, 6.0, -0.0, -0.5, -1.0, -1.5, -2.0, -3.0, -4.0, -6.0])


def pack_weight(w, fmt):
    k, n = w.shape
    w = f64(bf(w)).reshape(k // 32, 32, n)
    amax = np.abs(w).max(1)
    if fmt == "e4m3":
        byte = np.frexp(amax)[1] - 1 + 127 - 7
    else:
        mant, ex = np.frexp(amax / 6.0)
        byte = np.where(mant > 0.5, ex, ex - 1) + 127
    byte = np.clip(np.where(amax > 0, byte, 1), 1, 254)
    scaled = (w * np.exp2(127.0 - byte)[:, None, :]).reshape(k, n).astype(np.float32)
    by_word = np.ascontiguousarray(scaled.reshape(k // 512, 128, 4, n).transpose(0, 1, 3, 2))
    if fmt == "e4m3":
        words = by_word.astype(ml_dtypes.float8_e4m3fn).view(np.uint8)
    else:
        c = by_word.astype(ml_dtypes.float4_e2m1fn).view(np.uint8) & 0xF
        words = c[..., 0::2] | (c[..., 1::2] << 4)
    return np.ascontiguousarray(words), np.ascontiguousarray(byte.astype(np.uint8).reshape(k // 512, 16, n))


def unpack_weight(words, scales, fmt):
    g, p, n, _ = words.shape
    if fmt == "e4m3":
        vals = np.ascontiguousarray(words).view(ml_dtypes.float8_e4m3fn).astype(np.float64)
    else:
        nib = np.empty((g, p, n, 4), np.uint8)
        nib[..., 0::2] = words & 0xF
        nib[..., 1::2] = words >> 4
        vals = E2M1[nib]
    vals = vals * np.repeat(np.exp2(scales.astype(np.float64) - 127.0), 8, axis=1)[..., None]
    return vals.transpose(0, 1, 3, 2).reshape(g * 512, n)


B, G, C, D, E, S = 1, 1, 512, 640, 8192, 128
N = G * C


def setup_inputs():
    t = np.exp2(np.round(np.log2(mx_kscale(C)) * 0.5))
    r = mx_kscale(E)
    q_quad = bf(np.random.standard_normal((B, G, C, S)) * 0.57 / S ** 0.25)
    k_quad = bf(np.random.standard_normal((B, G, C, S)) * 0.57 / S ** 0.25 * t[:, None])
    q_lin = bf(np.random.standard_normal((B, G, C, S)) / np.sqrt(S))
    kv = bf(np.random.standard_normal((B, S, E)) * 0.15 * np.sqrt(N))
    v = bf(np.tanh(np.random.standard_normal((B, G, C, E))) / (t * t)[:, None])
    u = bf(np.tanh(np.random.standard_normal((B, G, C, E))) * r)
    rel_bias = bf(np.random.standard_normal(C) * 0.2 * t)
    Wod_words, Wod_scales = pack_weight(np.random.standard_normal((E, D)) * 0.5 / np.sqrt(E) / r[:, None], "e4m3")
    bod = bf(np.random.standard_normal(D) * 0.3)
    return {"q_quad": q_quad,
            "k_quad": k_quad,
            "q_lin": q_lin,
            "kv": kv,
            "v": v,
            "u": u,
            "rel_bias": rel_bias,
            "Wod_words": Wod_words,
            "Wod_scales": Wod_scales,
            "bod": bod}


def reference(q_quad, k_quad, q_lin, kv, v, u, rel_bias, Wod_words, Wod_scales, bod):
    qk = f64(q_quad) @ f64(k_quad).transpose(0, 1, 3, 2)
    a = np.square(np.maximum(qk + f64(rel_bias), 0.0))
    v_quad = mxq(a, 3, "e4m3") @ mxq(f64(v), 2, "e4m3")
    v_lin = (f64(q_lin).reshape(B, N, S) @ f64(kv)).reshape(B, G, C, E)
    h = f64(u) * (v_quad + v_lin)
    return (mxq(h, 3, "e4m3") @ unpack_weight(Wod_words, Wod_scales, "e4m3")) + f64(bod)

@@ -1,0 +1,312 @@
+from contextlib import ExitStack
+
+import concourse.mybir as mybir
+from concourse.masks import make_identity
+
+BF16 = mybir.dt.bfloat16
+F32 = mybir.dt.float32
+I32 = mybir.dt.int32
+U32 = mybir.dt.uint32
+U8 = mybir.dt.uint8
+FP8X4 = mybir.dt.float8_e4m3fn_x4
+ALU = mybir.AluOpType
+ACT = mybir.ActivationFunctionType
+
+P = 128
+PACK = 4
+K_PASS = P * PACK
+TOKENS = 512
+TOKEN_TILES = TOKENS // P
+HALF = TOKENS // 2
+S_DIM = 128
+E_DIM = 8192
+D_DIM = 640
+GROUPS = E_DIM // K_PASS
+CHUNK_GROUPS = 2
+CHUNK_E = CHUNK_GROUPS * K_PASS
+CHUNKS = GROUPS // CHUNK_GROUPS
+ROUND = 4
+ROUNDS = GROUPS // ROUND
+D_PARTS = ((0, 512), (512, 128))
+HALF_STEPS = 2 * GROUPS
+PROJECT_LAG = 10
+
+FLOPS = 2 * (TOKENS * TOKENS * S_DIM + TOKENS * TOKENS * E_DIM + TOKENS * S_DIM * E_DIM + TOKENS * E_DIM * D_DIM)
+
+
+def tile_flashattention_pa_k_kernel(
+    tc, q_quad, k_quad, q_lin, kv, v, u, rel_bias, Wod_words, Wod_scales, bod, out
+):
+    nc = tc.nc
+
+    q_rows = q_quad.flatten_outer_dims().rearrange("(p t) s -> p t s", t=TOKEN_TILES)
+    ql_rows = q_lin.flatten_outer_dims().rearrange("(p t) s -> p t s", t=TOKEN_TILES)
+    u_rows = u.flatten_outer_dims().rearrange("(p t) e -> p t e", t=TOKEN_TILES)
+    out_rows = out.flatten_outer_dims().rearrange("(p t) d -> p t d", t=TOKEN_TILES)
+    k_rows = k_quad.flatten_outer_dims().rearrange("(p j) s -> p j s", j=PACK)
+    v_rows = v.flatten_outer_dims().rearrange("(p j) e -> p j e", j=PACK)
+    kv_rows = kv.flatten_outer_dims()
+
+    with ExitStack() as stack:
+        stack.enter_context(tc.manual_schedule())
+        keep = stack.enter_context(tc.tile_pool(name="keep", bufs=1))
+        ring2 = stack.enter_context(tc.tile_pool(name="ring2", bufs=2))
+        ring3 = stack.enter_context(tc.tile_pool(name="ring3", bufs=3))
+
+        v_raw = {}
+        u_raw = {}
+        v_grouped = {}
+        v_codes = {}
+        v_plane = {}
+        sums = {}
+        vq_banks = {}
+        gate_banks = {}
+        h_grouped = {}
+        h_codes = {}
+        h_plane = {}
+        w_words = {}
+
+        def load_v(c):
+            v_raw[c] = ring3.tile([P, PACK, CHUNK_E], BF16, name="v_raw%d" % c, tag="v_raw")
+            nc.sync.dma_start(out=v_raw[c][:], in_=v_rows[:, :, c * CHUNK_E : (c + 1) * CHUNK_E])
+
+        def load_u(c):
+            u_raw[c] = ring3.tile([P, TOKEN_TILES, CHUNK_E], BF16, name="u_raw%d" % c, tag="u_raw")
+            nc.sync.dma_start(out=u_raw[c][:], in_=u_rows[:, :, c * CHUNK_E : (c + 1) * CHUNK_E])
+
+        def load_kv(quarter):
+            cols = slice(quarter * ROUND * K_PASS, (quarter + 1) * ROUND * K_PASS)
+            nc.sync.dma_start(out=kv_sb[:, cols], in_=kv_rows[:, cols])
+
+        def load_w_words(r):
+            w_words[r] = ring2.tile([P, ROUND, D_DIM], U32, name="w_words%d" % r, tag="w_words", align_bytes=64)
+            nc.sync.dma_start(
+                out=w_words[r][:].bitcast(I32),
+                in_=Wod_words[r * ROUND : (r + 1) * ROUND].rearrange("g p n t -> p g (n t)").bitcast(I32),
+            )
+
+        def load_w_scales():
+            for quadrant in range(4):
+                nc.sync.dma_start(
+                    out=w_planes[32 * quadrant : 32 * quadrant + 4, :, :].bitcast(I32),
+                    in_=Wod_scales[:, 4 * quadrant : 4 * quadrant + 4, :].rearrange("g r n -> r g n").bitcast(I32),
+                )
+
+        ident_bf = keep.tile([P, P], BF16)
+        make_identity(nc, ident_bf[:])
+        ident_f32 = keep.tile([P, P], F32)
+        make_identity(nc, ident_f32[:])
+        w_planes = keep.tile([P, GROUPS, D_DIM], U8, align_bytes=64)
+        nc.vector.memset(w_planes[:].bitcast(I32), 0)
+
+        k_sb = keep.tile([P, PACK, S_DIM], BF16)
+        nc.sync.dma_start(out=k_sb[:], in_=k_rows)
+        q_sb = keep.tile([P, TOKEN_TILES, S_DIM], BF16)
+        nc.sync.dma_start(out=q_sb[:], in_=q_rows)
+        bias_bf = keep.tile([P, PACK], BF16)
+        nc.sync.dma_start(out=bias_bf[:], in_=rel_bias.rearrange("(p j) -> p j", j=PACK))
+        load_v(0)
+        ql_sb = keep.tile([P, TOKEN_TILES, S_DIM], BF16)
+        nc.sync.dma_start(out=ql_sb[:], in_=ql_rows)
+        kv_sb = keep.tile([P, E_DIM], BF16)
+        load_kv(0)
+        load_u(0)
+        load_v(1)
+        load_u(1)
+
+        def regroup(copy, g, first_p, last_p):
+            c, lo = g // CHUNK_GROUPS, (g % CHUNK_GROUPS) * K_PASS
+            if first_p == 0:
+                v_grouped[g] = ring2.tile([P, PACK, P, PACK], BF16, name="v_grouped%d" % g, tag="v_grouped", align_bytes=64)
+            copy(
+                out=v_grouped[g][:].rearrange("q t p j -> q p j t")[:, first_p:last_p],
+                in_=v_raw[c][:, :, lo : lo + K_PASS].rearrange("q j (p t) -> q p j t", t=PACK)[:, first_p:last_p],
+            )
+
+        def quantise_v(g):
+            v_codes[g] = ring3.tile([P, K_PASS], U32, name="v_codes%d" % g, tag="v_codes", align_bytes=64)
+            v_plane[g] = ring3.tile([P, K_PASS], U8, name="v_plane%d" % g, tag="v_plane", align_bytes=64)
+            nc.vector.quantize_mx(
+                out=v_codes[g][:].bitcast(FP8X4),
+                scales=v_plane[g][:],
+                in_=v_grouped[g][:].rearrange("q t p j -> q (t p j)"),
+            )
+
+        kT = keep.tile([P, PACK, P], BF16)
+        qT = keep.tile([P, TOKEN_TILES, P], BF16)
+        qlT = keep.tile([P, TOKEN_TILES, P], BF16)
+        bias_f32 = keep.tile([P, PACK], F32)
+        relu = keep.tile([P, PACK, TOKENS], F32)
+        a_grouped = keep.tile([P, TOKENS, PACK], BF16, align_bytes=64)
+        a_codes = keep.tile([P, TOKENS], U32, align_bytes=64)
+        a_plane = keep.tile([P, TOKENS], U8, align_bytes=64)
+
+        with tc.psum_pool(name="head_psum", bufs=1) as head_psum:
+            nc.vector.tensor_copy(out=bias_f32[:], in_=bias_bf[:])
+            kT_ps = head_psum.tile([P, PACK, P], BF16)
+            for j in range(PACK):
+                nc.tensor.transpose(kT_ps[:, j, :], k_sb[:, j, :], ident_bf[:])
+            nc.vector.tensor_copy(out=kT[:], in_=kT_ps[:])
+            qT_ps = head_psum.tile([P, TOKEN_TILES, P], BF16)
+            for t in range(TOKEN_TILES):
+                nc.tensor.transpose(qT_ps[:, t, :], q_sb[:, t, :], ident_bf[:])
+            nc.scalar.copy(out=qT[:], in_=qT_ps[:])
+            for j in range(PACK):
+                qk_ps = head_psum.tile([P, TOKENS], F32, name="qk_ps%d" % j)
+                nc.tensor.matmul(
+                    qk_ps[:], lhsT=kT[:, j, :], rhs=qT[:].rearrange("s t p -> s (t p)"), start=True, stop=True
+                )
+                if j % 2 == 0:
+                    nc.scalar.activation(out=relu[:, j, :], in_=qk_ps[:], func=ACT.Relu, bias=bias_f32[:, j : j + 1])
+                else:
+                    nc.vector.tensor_scalar(
+                        out=relu[:, j, :], in0=qk_ps[:], scalar1=bias_f32[:, j : j + 1], scalar2=0.0,
+                        op0=ALU.add, op1=ALU.max,
+                    )
+            qlT_ps = head_psum.tile([P, TOKEN_TILES, P], BF16)
+            for t in range(TOKEN_TILES):
+                nc.tensor.transpose(qlT_ps[:, t, :], ql_sb[:, t, :], ident_bf[:])
+            nc.scalar.activation(
+                out=a_grouped[:, 0:HALF, :], in_=relu[:, :, 0:HALF].rearrange("p j c -> p c j"), func=ACT.Square
+            )
+            nc.vector.tensor_tensor(
+                out=a_grouped[:, HALF:TOKENS, :],
+                in0=relu[:, :, HALF:TOKENS].rearrange("p j c -> p c j"),
+                in1=relu[:, :, HALF:TOKENS].rearrange("p j c -> p c j"),
+                op=ALU.mult,
+            )
+            nc.scalar.copy(out=qlT[:], in_=qlT_ps[:])
+            regroup(nc.vector.tensor_copy, 0, 0, P)
+            nc.vector.quantize_mx(
+                out=a_codes[:].bitcast(FP8X4), scales=a_plane[:], in_=a_grouped[:].rearrange("p c j -> p (c j)")
+            )
+            regroup(nc.vector.tensor_copy, 1, 0, P)
+            quantise_v(0)
+
+        acc = keep.tile([P, TOKEN_TILES, D_DIM], F32)
+        bod_bc = keep.tile([P, D_DIM], BF16)
+
+        psum = stack.enter_context(tc.psum_pool(name="psum", bufs=2))
+
+        def sums_matmuls(k):
+            n, h = k // 2, k % 2
+            if h == 0:
+                sums[n] = ring3.tile([P, PACK, TOKENS], F32, name="sums%d" % n, tag="sums")
+            for t in (2 * h, 2 * h + 1):
+                vl_ps = psum.tile([P, TOKENS], F32, name="vl_ps", tag="vl")
+                nc.tensor.matmul(
+                    vl_ps[:],
+                    lhsT=kv_sb[:, n * K_PASS + t : (n + 1) * K_PASS : PACK],
+                    rhs=qlT[:].rearrange("s t p -> s (t p)"),
+                    start=True,
+                    stop=True,
+                )
+                nc.scalar.copy(out=sums[n][:, t, :], in_=vl_ps[:])
+                vq_banks[(n, t)] = psum.tile([P, TOKENS], F32, name="vq_ps", tag="vq")
+                nc.tensor.matmul_mx(
+                    out=vq_banks[(n, t)][:],
+                    lhsT=v_codes[n][:, t * P : (t + 1) * P].bitcast(FP8X4),
+                    lhsT_scale=v_plane[n][:, t * P : (t + 1) * P],
+                    rhs=a_codes[:].bitcast(FP8X4),
+                    rhs_scale=a_plane[:],
+                    start=True,
+                    stop=True,
+                )
+                if n + 2 < GROUPS:
+                    regroup(nc.scalar.copy, n + 2, t * (P // PACK), (t + 1) * (P // PACK))
+
+        def add_sums(k):
+            n, h = k // 2, k % 2
+            for t in (2 * h, 2 * h + 1):
+                nc.vector.tensor_tensor(out=sums[n][:, t, :], in0=vq_banks[(n, t)][:], in1=sums[n][:, t, :], op=ALU.add)
+
+        def transpose_gate(k):
+            n, h = k // 2, k % 2
+            c, lo = n // CHUNK_GROUPS, (n % CHUNK_GROUPS) * K_PASS
+            gate_banks[k] = psum.tile([P, 2, HALF], F32, name="gate_ps", tag="gate")
+            for tile_in_half in range(2):
+                words = u_raw[c][:, 2 * h + tile_in_half, lo : lo + K_PASS].bitcast(F32)
+                for pair in range(2):
+                    nc.tensor.transpose(
+                        gate_banks[k][:, pair, tile_in_half * P : (tile_in_half + 1) * P],
+                        words[:, pair : K_PASS // 2 : 2],
+                        ident_f32[:],
+                    )
+
+        def gate(k):
+            n, h = k // 2, k % 2
+            if h == 0:
+                h_grouped[n] = ring2.tile([P, TOKENS, PACK], BF16, name="h_grouped%d" % n, tag="h_grouped", align_bytes=64)
+            cols = slice(h * HALF, (h + 1) * HALF)
+            nc.vector.tensor_tensor(
+                out=h_grouped[n][:, cols, :].rearrange("p c (w e) -> p c w e", w=2),
+                in0=sums[n][:, :, cols].rearrange("p (w e) c -> p c w e", w=2),
+                in1=gate_banks[k][:].bitcast(BF16).rearrange("p w (c e) -> p c w e", e=2),
+                op=ALU.mult,
+            )
+
+        def quantise_h(n):
+            r, g = n // ROUND, n % ROUND
+            if g == 0:
+                h_codes[r] = ring2.tile([P, ROUND, TOKENS], U32, name="h_codes%d" % r, tag="h_codes", align_bytes=64)
+                h_plane[r] = ring2.tile([P, ROUND, TOKENS], U8, name="h_plane%d" % r, tag="h_plane", align_bytes=64)
+            nc.vector.quantize_mx(
+                out=h_codes[r][:, g, :].bitcast(FP8X4),
+                scales=h_plane[r][:, g, :],
+                in_=h_grouped[n][:].rearrange("p c t -> p (c t)"),
+            )
+
+        def project(index):
+            r, tile_and_part = index // (2 * TOKEN_TILES), index % (2 * TOKEN_TILES)
+            t, part = tile_and_part // 2, tile_and_part % 2
+            first, width = D_PARTS[part]
+            proj_ps = psum.tile([P, 512], F32, name="proj_ps", tag="proj")
+            for g in range(ROUND):
+                nc.tensor.matmul_mx(
+                    out=proj_ps[:, 0:width],
+                    lhsT=h_codes[r][:, g, t * P : (t + 1) * P].bitcast(FP8X4),
+                    lhsT_scale=h_plane[r][:, g, t * P : (t + 1) * P],
+                    rhs=w_words[r][:, g, first : first + width].bitcast(FP8X4),
+                    rhs_scale=w_planes[:, r * ROUND + g, first : first + width],
+                    start=(g == 0),
+                    stop=(g == ROUND - 1),
+                )
+            target = acc[:, t, first : first + width]
+            if r < ROUNDS - 1:
+                partial = ring2.tile([P, 512], F32, name="partial", tag="partial")
+                nc.scalar.copy(out=partial[:, 0:width], in_=proj_ps[:, 0:width])
+                nc.gpsimd.tensor_tensor(out=target, in0=target, in1=partial[:, 0:width], op=ALU.add)
+            else:
+                nc.vector.tensor_tensor(out=target, in0=proj_ps[:, 0:width], in1=target, op=ALU.add)
+                if part == 1:
+                    nc.sync.dma_start(out=out_rows[:, t, :], in_=acc[:, t, :])
+
+        for k in range(-1, ROUNDS * 2 * TOKEN_TILES + PROJECT_LAG):
+            n, h = k // 2, k % 2
+            if h == 0 and 0 <= n < GROUPS:
+                if n % 2 == 0 and n // 2 + 2 < CHUNKS:
+                    load_v(n // 2 + 2)
+                    load_u(n // 2 + 2)
+                if n % ROUND == 0 and n // ROUND + 1 < ROUNDS:
+                    load_kv(n // ROUND + 1)
+                if n % ROUND == 2:
+                    load_w_words(n // ROUND)
+                if n == 1:
+                    load_w_scales()
+                    nc.sync.dma_start(out=bod_bc[:], in_=bod.partition_broadcast(P))
+                    for t in range(TOKEN_TILES):
+                        nc.gpsimd.tensor_copy(out=acc[:, t, :], in_=bod_bc[:])
+            if 0 <= k - 2 < HALF_STEPS:
+                gate(k - 2)
+            if 0 <= k + 1 < HALF_STEPS:
+                sums_matmuls(k + 1)
+            if 0 <= k < HALF_STEPS:
+                add_sums(k)
+            if 0 <= k - PROJECT_LAG:
+                project(k - PROJECT_LAG)
+            if 0 <= k < HALF_STEPS:
+                transpose_gate(k)
+            if h == 0 and 0 <= n and n + 1 < GROUPS:
+                quantise_v(n + 1)
+            if h == 1 and 0 <= n - 1 < GROUPS:
+                quantise_h(n - 1)

@@ -114,13 +114,13 @@ def tile_flashattention_pa_k_kernel(
         load_v(1)
         load_u(1)
 
-        def regroup(copy, g, first_p, last_p):
+        def regroup(copy, g, first_t, last_t):
             c, lo = g // CHUNK_GROUPS, (g % CHUNK_GROUPS) * K_PASS
-            if first_p == 0:
+            if first_t == 0:
                 v_grouped[g] = ring2.tile([P, PACK, P, PACK], BF16, name="v_grouped%d" % g, tag="v_grouped", align_bytes=64)
             copy(
-                out=v_grouped[g][:].rearrange("q t p j -> q p j t")[:, first_p:last_p],
-                in_=v_raw[c][:, :, lo : lo + K_PASS].rearrange("q j (p t) -> q p j t", t=PACK)[:, first_p:last_p],
+                out=v_grouped[g][:, first_t:last_t],
+                in_=v_raw[c][:, :, lo : lo + K_PASS].rearrange("q j (p t) -> q t p j", t=PACK)[:, first_t:last_t],
             )
 
         def quantise_v(g):
@@ -176,11 +176,11 @@ def tile_flashattention_pa_k_kernel(
                 op=ALU.mult,
             )
             nc.scalar.copy(out=qlT[:], in_=qlT_ps[:])
-            regroup(nc.vector.tensor_copy, 0, 0, P)
+            regroup(nc.vector.tensor_copy, 0, 0, PACK)
             nc.vector.quantize_mx(
                 out=a_codes[:].bitcast(FP8X4), scales=a_plane[:], in_=a_grouped[:].rearrange("p c j -> p (c j)")
             )
-            regroup(nc.vector.tensor_copy, 1, 0, P)
+            regroup(nc.vector.tensor_copy, 1, 0, PACK)
             quantise_v(0)
 
         acc = keep.tile([P, TOKEN_TILES, D_DIM], F32)
@@ -213,7 +213,7 @@ def tile_flashattention_pa_k_kernel(
                     stop=True,
                 )
                 if n + 2 < GROUPS:
-                    regroup(nc.scalar.copy, n + 2, t * (P // PACK), (t + 1) * (P // PACK))
+                    regroup(nc.scalar.copy, n + 2, t, t + 1)
 
         def add_sums(k):
             n, h = k // 2, k % 2

@@ -213,7 +213,7 @@ def tile_flashattention_pa_k_kernel(
                     stop=True,
                 )
                 if n + 2 < GROUPS:
-                    regroup(nc.scalar.copy, n + 2, t, t + 1)
+                    regroup(nc.scalar.copy if t % 2 == 0 else nc.vector.tensor_copy, n + 2, t, t + 1)
 
         def add_sums(k):
             n, h = k // 2, k % 2

@@ -29,6 +29,7 @@ ROUND = 4
 ROUNDS = GROUPS // ROUND
 D_PARTS = ((0, 512), (512, 128))
 HALF_STEPS = 2 * GROUPS
+LAST_ROUND_BANKS = ("proj", "vl", "vq", "gate")
 PROJECT_LAG = 10
 
 FLOPS = 2 * (TOKENS * TOKENS * S_DIM + TOKENS * TOKENS * E_DIM + TOKENS * S_DIM * E_DIM + TOKENS * E_DIM * D_DIM)
@@ -103,11 +104,11 @@ def tile_flashattention_pa_k_kernel(
         nc.sync.dma_start(out=k_sb[:], in_=k_rows)
         q_sb = keep.tile([P, TOKEN_TILES, S_DIM], BF16)
         nc.sync.dma_start(out=q_sb[:], in_=q_rows)
+        ql_sb = keep.tile([P, TOKEN_TILES, S_DIM], BF16)
+        nc.sync.dma_start(out=ql_sb[:], in_=ql_rows)
         bias_bf = keep.tile([P, PACK], BF16)
         nc.sync.dma_start(out=bias_bf[:], in_=rel_bias.rearrange("(p j) -> p j", j=PACK))
         load_v(0)
-        ql_sb = keep.tile([P, TOKEN_TILES, S_DIM], BF16)
-        nc.sync.dma_start(out=ql_sb[:], in_=ql_rows)
         kv_sb = keep.tile([P, E_DIM], BF16)
         load_kv(0)
         load_u(0)
@@ -141,6 +142,9 @@ def tile_flashattention_pa_k_kernel(
         a_codes = keep.tile([P, TOKENS], U32, align_bytes=64)
         a_plane = keep.tile([P, TOKENS], U8, align_bytes=64)
 
+        def gpsimd_copy(out, in_):
+            nc.gpsimd.tensor_scalar(out=out, in0=in_, scalar1=1.0, scalar2=0.0, op0=ALU.mult, op1=ALU.add)
+
         with tc.psum_pool(name="head_psum", bufs=1) as head_psum:
             nc.vector.tensor_copy(out=bias_f32[:], in_=bias_bf[:])
             kT_ps = head_psum.tile([P, PACK, P], BF16)
@@ -151,21 +155,20 @@ def tile_flashattention_pa_k_kernel(
             for t in range(TOKEN_TILES):
                 nc.tensor.transpose(qT_ps[:, t, :], q_sb[:, t, :], ident_bf[:])
             nc.scalar.copy(out=qT[:], in_=qT_ps[:])
+            qlT_ps = head_psum.tile([P, TOKEN_TILES, P], BF16)
+            for t in range(TOKEN_TILES):
+                nc.tensor.transpose(qlT_ps[:, t, :], ql_sb[:, t, :], ident_bf[:])
+            nc.vector.tensor_copy(out=qlT[:], in_=qlT_ps[:])
+            regroup(nc.vector.tensor_copy, 0, 0, PACK)
+            quantise_v(0)
+            for t in range(PACK):
+                regroup(gpsimd_copy, 1, t, t + 1)
             for j in range(PACK):
                 qk_ps = head_psum.tile([P, TOKENS], F32, name="qk_ps%d" % j)
                 nc.tensor.matmul(
                     qk_ps[:], lhsT=kT[:, j, :], rhs=qT[:].rearrange("s t p -> s (t p)"), start=True, stop=True
                 )
-                if j % 2 == 0:
-                    nc.scalar.activation(out=relu[:, j, :], in_=qk_ps[:], func=ACT.Relu, bias=bias_f32[:, j : j + 1])
-                else:
-                    nc.vector.tensor_scalar(
-                        out=relu[:, j, :], in0=qk_ps[:], scalar1=bias_f32[:, j : j + 1], scalar2=0.0,
-                        op0=ALU.add, op1=ALU.max,
-                    )
-            qlT_ps = head_psum.tile([P, TOKEN_TILES, P], BF16)
-            for t in range(TOKEN_TILES):
-                nc.tensor.transpose(qlT_ps[:, t, :], ql_sb[:, t, :], ident_bf[:])
+                nc.scalar.activation(out=relu[:, j, :], in_=qk_ps[:], func=ACT.Relu, bias=bias_f32[:, j : j + 1])
             nc.scalar.activation(
                 out=a_grouped[:, 0:HALF, :], in_=relu[:, :, 0:HALF].rearrange("p j c -> p c j"), func=ACT.Square
             )
@@ -175,13 +178,9 @@ def tile_flashattention_pa_k_kernel(
                 in1=relu[:, :, HALF:TOKENS].rearrange("p j c -> p c j"),
                 op=ALU.mult,
             )
-            nc.scalar.copy(out=qlT[:], in_=qlT_ps[:])
-            regroup(nc.vector.tensor_copy, 0, 0, PACK)
             nc.vector.quantize_mx(
                 out=a_codes[:].bitcast(FP8X4), scales=a_plane[:], in_=a_grouped[:].rearrange("p c j -> p (c j)")
             )
-            regroup(nc.vector.tensor_copy, 1, 0, PACK)
-            quantise_v(0)
 
         acc = keep.tile([P, TOKEN_TILES, D_DIM], F32)
         bod_bc = keep.tile([P, D_DIM], BF16)
@@ -213,7 +212,7 @@ def tile_flashattention_pa_k_kernel(
                     stop=True,
                 )
                 if n + 2 < GROUPS:
-                    regroup(nc.scalar.copy if t % 2 == 0 else nc.vector.tensor_copy, n + 2, t, t + 1)
+                    regroup(nc.scalar.copy, n + 2, t, t + 1)
 
         def add_sums(k):
             n, h = k // 2, k % 2
@@ -260,7 +259,8 @@ def tile_flashattention_pa_k_kernel(
             r, tile_and_part = index // (2 * TOKEN_TILES), index % (2 * TOKEN_TILES)
             t, part = tile_and_part // 2, tile_and_part % 2
             first, width = D_PARTS[part]
-            proj_ps = psum.tile([P, 512], F32, name="proj_ps", tag="proj")
+            bank = LAST_ROUND_BANKS[tile_and_part % len(LAST_ROUND_BANKS)] if r == ROUNDS - 1 else "proj"
+            proj_ps = psum.tile([P, 512], F32, name="proj_ps", tag=bank)
             for g in range(ROUND):
                 nc.tensor.matmul_mx(
                     out=proj_ps[:, 0:width],
@@ -275,7 +275,8 @@ def tile_flashattention_pa_k_kernel(
             if r < ROUNDS - 1:
                 partial = ring2.tile([P, 512], F32, name="partial", tag="partial")
                 nc.scalar.copy(out=partial[:, 0:width], in_=proj_ps[:, 0:width])
-                nc.gpsimd.tensor_tensor(out=target, in0=target, in1=partial[:, 0:width], op=ALU.add)
+                so_far = bod_bc[:, first : first + width] if r == 0 else target
+                nc.gpsimd.tensor_tensor(out=target, in0=so_far, in1=partial[:, 0:width], op=ALU.add)
             else:
                 nc.vector.tensor_tensor(out=target, in0=proj_ps[:, 0:width], in1=target, op=ALU.add)
                 if part == 1:
@@ -294,8 +295,6 @@ def tile_flashattention_pa_k_kernel(
                 if n == 1:
                     load_w_scales()
                     nc.sync.dma_start(out=bod_bc[:], in_=bod.partition_broadcast(P))
-                    for t in range(TOKEN_TILES):
-                        nc.gpsimd.tensor_copy(out=acc[:, t, :], in_=bod_bc[:])
             if 0 <= k - 2 < HALF_STEPS:
                 gate(k - 2)
             if 0 <= k + 1 < HALF_STEPS:

@@ -189,35 +189,44 @@ def tile_flashattention_pa_k_kernel(
 
         def sums_matmuls(k):
             n, h = k // 2, k % 2
+            cols = slice(h * HALF, (h + 1) * HALF)
             if h == 0:
-                sums[n] = ring3.tile([P, PACK, TOKENS], F32, name="sums%d" % n, tag="sums")
-            for t in (2 * h, 2 * h + 1):
-                vl_ps = psum.tile([P, TOKENS], F32, name="vl_ps", tag="vl")
-                nc.tensor.matmul(
-                    vl_ps[:],
-                    lhsT=kv_sb[:, n * K_PASS + t : (n + 1) * K_PASS : PACK],
-                    rhs=qlT[:].rearrange("s t p -> s (t p)"),
-                    start=True,
-                    stop=True,
-                )
-                nc.scalar.copy(out=sums[n][:, t, :], in_=vl_ps[:])
-                vq_banks[(n, t)] = psum.tile([P, TOKENS], F32, name="vq_ps", tag="vq")
-                nc.tensor.matmul_mx(
-                    out=vq_banks[(n, t)][:],
-                    lhsT=v_codes[n][:, t * P : (t + 1) * P].bitcast(FP8X4),
-                    lhsT_scale=v_plane[n][:, t * P : (t + 1) * P],
-                    rhs=a_codes[:].bitcast(FP8X4),
-                    rhs_scale=a_plane[:],
-                    start=True,
-                    stop=True,
-                )
+                sums[n] = ring3.tile([P, 2, 2, HALF, 2], F32, name="sums%d" % n, tag="sums")
+            for w in range(2):
+                vl_ps = psum.tile([P, 2, HALF], F32, name="vl_ps", tag="vl")
+                for e in range(2):
+                    nc.tensor.matmul(
+                        vl_ps[:, e, :],
+                        lhsT=kv_sb[:, n * K_PASS + 2 * w + e : (n + 1) * K_PASS : PACK],
+                        rhs=qlT[:].rearrange("s t p -> s (t p)")[:, cols],
+                        start=True,
+                        stop=True,
+                    )
+                nc.scalar.copy(out=sums[n][:, h, w], in_=vl_ps[:].rearrange("p e c -> p c e"))
+                vq_banks[(k, w)] = psum.tile([P, 2, HALF], F32, name="vq_ps", tag="vq")
+                for e in range(2):
+                    t = 2 * w + e
+                    nc.tensor.matmul_mx(
+                        out=vq_banks[(k, w)][:, e, :],
+                        lhsT=v_codes[n][:, t * P : (t + 1) * P].bitcast(FP8X4),
+                        lhsT_scale=v_plane[n][:, t * P : (t + 1) * P],
+                        rhs=a_codes[:, cols].bitcast(FP8X4),
+                        rhs_scale=a_plane[:, cols],
+                        start=True,
+                        stop=True,
+                    )
                 if n + 2 < GROUPS:
-                    regroup(nc.scalar.copy, n + 2, t, t + 1)
+                    regroup(nc.scalar.copy, n + 2, 2 * h + w, 2 * h + w + 1)
 
         def add_sums(k):
             n, h = k // 2, k % 2
-            for t in (2 * h, 2 * h + 1):
-                nc.vector.tensor_tensor(out=sums[n][:, t, :], in0=vq_banks[(n, t)][:], in1=sums[n][:, t, :], op=ALU.add)
+            for w in range(2):
+                nc.vector.tensor_tensor(
+                    out=sums[n][:, h, w],
+                    in0=vq_banks[(k, w)][:].rearrange("p e c -> p c e"),
+                    in1=sums[n][:, h, w],
+                    op=ALU.add,
+                )
 
         def transpose_gate(k):
             n, h = k // 2, k % 2
@@ -239,7 +248,7 @@ def tile_flashattention_pa_k_kernel(
             cols = slice(h * HALF, (h + 1) * HALF)
             nc.vector.tensor_tensor(
                 out=h_grouped[n][:, cols, :].rearrange("p c (w e) -> p c w e", w=2),
-                in0=sums[n][:, :, cols].rearrange("p (w e) c -> p c w e", w=2),
+                in0=sums[n][:, h].rearrange("p w c e -> p c w e"),
                 in1=gate_banks[k][:].bitcast(BF16).rearrange("p w (c e) -> p c w e", e=2),
                 op=ALU.mult,
             )

from contextlib import ExitStack

import concourse.mybir as mybir
from concourse.masks import make_identity

BF16 = mybir.dt.bfloat16
F32 = mybir.dt.float32
I32 = mybir.dt.int32
U32 = mybir.dt.uint32
U8 = mybir.dt.uint8
FP8X4 = mybir.dt.float8_e4m3fn_x4
ALU = mybir.AluOpType
ACT = mybir.ActivationFunctionType

P = 128
PACK = 4
K_PASS = P * PACK
TOKENS = 512
TOKEN_TILES = TOKENS // P
HALF = TOKENS // 2
S_DIM = 128
E_DIM = 8192
D_DIM = 640
GROUPS = E_DIM // K_PASS
CHUNK_GROUPS = 2
CHUNK_E = CHUNK_GROUPS * K_PASS
CHUNKS = GROUPS // CHUNK_GROUPS
ROUND = 4
ROUNDS = GROUPS // ROUND
D_PARTS = ((0, 512), (512, 128))
HALF_STEPS = 2 * GROUPS
LAST_ROUND_BANKS = ("proj", "vl", "vq", "gate")
PROJECT_LAG = 10

FLOPS = 2 * (TOKENS * TOKENS * S_DIM + TOKENS * TOKENS * E_DIM + TOKENS * S_DIM * E_DIM + TOKENS * E_DIM * D_DIM)


def tile_flashattention_pa_k_kernel(
    tc, q_quad, k_quad, q_lin, kv, v, u, rel_bias, Wod_words, Wod_scales, bod, out
):
    nc = tc.nc

    q_rows = q_quad.flatten_outer_dims().rearrange("(p t) s -> p t s", t=TOKEN_TILES)
    ql_rows = q_lin.flatten_outer_dims().rearrange("(p t) s -> p t s", t=TOKEN_TILES)
    u_rows = u.flatten_outer_dims().rearrange("(p t) e -> p t e", t=TOKEN_TILES)
    out_rows = out.flatten_outer_dims().rearrange("(p t) d -> p t d", t=TOKEN_TILES)
    k_rows = k_quad.flatten_outer_dims().rearrange("(p j) s -> p j s", j=PACK)
    v_rows = v.flatten_outer_dims().rearrange("(p j) e -> p j e", j=PACK)
    kv_rows = kv.flatten_outer_dims()

    with ExitStack() as stack:
        stack.enter_context(tc.manual_schedule())
        keep = stack.enter_context(tc.tile_pool(name="keep", bufs=1))
        ring2 = stack.enter_context(tc.tile_pool(name="ring2", bufs=2))
        ring3 = stack.enter_context(tc.tile_pool(name="ring3", bufs=3))

        v_raw = {}
        u_raw = {}
        v_grouped = {}
        v_codes = {}
        v_plane = {}
        sums = {}
        vq_banks = {}
        gate_banks = {}
        h_grouped = {}
        h_codes = {}
        h_plane = {}
        w_words = {}

        def load_v(c):
            v_raw[c] = ring3.tile([P, PACK, CHUNK_E], BF16, name="v_raw%d" % c, tag="v_raw")
            nc.sync.dma_start(out=v_raw[c][:], in_=v_rows[:, :, c * CHUNK_E : (c + 1) * CHUNK_E])

        def load_u(c):
            u_raw[c] = ring3.tile([P, TOKEN_TILES, CHUNK_E], BF16, name="u_raw%d" % c, tag="u_raw")
            nc.sync.dma_start(out=u_raw[c][:], in_=u_rows[:, :, c * CHUNK_E : (c + 1) * CHUNK_E])

        def load_kv(quarter):
            cols = slice(quarter * ROUND * K_PASS, (quarter + 1) * ROUND * K_PASS)
            nc.sync.dma_start(out=kv_sb[:, cols], in_=kv_rows[:, cols])

        def load_w_words(r):
            w_words[r] = ring2.tile([P, ROUND, D_DIM], U32, name="w_words%d" % r, tag="w_words", align_bytes=64)
            nc.sync.dma_start(
                out=w_words[r][:].bitcast(I32),
                in_=Wod_words[r * ROUND : (r + 1) * ROUND].rearrange("g p n t -> p g (n t)").bitcast(I32),
            )

        def load_w_scales():
            for quadrant in range(4):
                nc.sync.dma_start(
                    out=w_planes[32 * quadrant : 32 * quadrant + 4, :, :].bitcast(I32),
                    in_=Wod_scales[:, 4 * quadrant : 4 * quadrant + 4, :].rearrange("g r n -> r g n").bitcast(I32),
                )

        ident_bf = keep.tile([P, P], BF16)
        make_identity(nc, ident_bf[:])
        ident_f32 = keep.tile([P, P], F32)
        make_identity(nc, ident_f32[:])
        w_planes = keep.tile([P, GROUPS, D_DIM], U8, align_bytes=64)
        nc.vector.memset(w_planes[:].bitcast(I32), 0)

        k_sb = keep.tile([P, PACK, S_DIM], BF16)
        nc.sync.dma_start(out=k_sb[:], in_=k_rows)
        q_sb = keep.tile([P, TOKEN_TILES, S_DIM], BF16)
        nc.sync.dma_start(out=q_sb[:], in_=q_rows)
        ql_sb = keep.tile([P, TOKEN_TILES, S_DIM], BF16)
        nc.sync.dma_start(out=ql_sb[:], in_=ql_rows)
        bias_bf = keep.tile([P, PACK], BF16)
        nc.sync.dma_start(out=bias_bf[:], in_=rel_bias.rearrange("(p j) -> p j", j=PACK))
        load_v(0)
        kv_sb = keep.tile([P, E_DIM], BF16)
        load_kv(0)
        load_u(0)
        load_v(1)
        load_u(1)

        def regroup(copy, g, first_t, last_t):
            c, lo = g // CHUNK_GROUPS, (g % CHUNK_GROUPS) * K_PASS
            if first_t == 0:
                v_grouped[g] = ring2.tile([P, PACK, P, PACK], BF16, name="v_grouped%d" % g, tag="v_grouped", align_bytes=64)
            copy(
                out=v_grouped[g][:, first_t:last_t],
                in_=v_raw[c][:, :, lo : lo + K_PASS].rearrange("q j (p t) -> q t p j", t=PACK)[:, first_t:last_t],
            )

        def quantise_v(g):
            v_codes[g] = ring3.tile([P, K_PASS], U32, name="v_codes%d" % g, tag="v_codes", align_bytes=64)
            v_plane[g] = ring3.tile([P, K_PASS], U8, name="v_plane%d" % g, tag="v_plane", align_bytes=64)
            nc.vector.quantize_mx(
                out=v_codes[g][:].bitcast(FP8X4),
                scales=v_plane[g][:],
                in_=v_grouped[g][:].rearrange("q t p j -> q (t p j)"),
            )

        kT = keep.tile([P, PACK, P], BF16)
        qT = keep.tile([P, TOKEN_TILES, P], BF16)
        qlT = keep.tile([P, TOKEN_TILES, P], BF16)
        bias_f32 = keep.tile([P, PACK], F32)
        relu = keep.tile([P, PACK, TOKENS], F32)
        a_grouped = keep.tile([P, TOKENS, PACK], BF16, align_bytes=64)
        a_codes = keep.tile([P, TOKENS], U32, align_bytes=64)
        a_plane = keep.tile([P, TOKENS], U8, align_bytes=64)

        def gpsimd_copy(out, in_):
            nc.gpsimd.tensor_scalar(out=out, in0=in_, scalar1=1.0, scalar2=0.0, op0=ALU.mult, op1=ALU.add)

        with tc.psum_pool(name="head_psum", bufs=1) as head_psum:
            nc.vector.tensor_copy(out=bias_f32[:], in_=bias_bf[:])
            kT_ps = head_psum.tile([P, PACK, P], BF16)
            for j in range(PACK):
                nc.tensor.transpose(kT_ps[:, j, :], k_sb[:, j, :], ident_bf[:])
            nc.vector.tensor_copy(out=kT[:], in_=kT_ps[:])
            qT_ps = head_psum.tile([P, TOKEN_TILES, P], BF16)
            for t in range(TOKEN_TILES):
                nc.tensor.transpose(qT_ps[:, t, :], q_sb[:, t, :], ident_bf[:])
            nc.scalar.copy(out=qT[:], in_=qT_ps[:])
            qlT_ps = head_psum.tile([P, TOKEN_TILES, P], BF16)
            for t in range(TOKEN_TILES):
                nc.tensor.transpose(qlT_ps[:, t, :], ql_sb[:, t, :], ident_bf[:])
            nc.vector.tensor_copy(out=qlT[:], in_=qlT_ps[:])
            regroup(nc.vector.tensor_copy, 0, 0, PACK)
            quantise_v(0)
            for t in range(PACK):
                regroup(gpsimd_copy, 1, t, t + 1)
            for j in range(PACK):
                qk_ps = head_psum.tile([P, TOKENS], F32, name="qk_ps%d" % j)
                nc.tensor.matmul(
                    qk_ps[:], lhsT=kT[:, j, :], rhs=qT[:].rearrange("s t p -> s (t p)"), start=True, stop=True
                )
                nc.scalar.activation(out=relu[:, j, :], in_=qk_ps[:], func=ACT.Relu, bias=bias_f32[:, j : j + 1])
            nc.scalar.activation(
                out=a_grouped[:, 0:HALF, :], in_=relu[:, :, 0:HALF].rearrange("p j c -> p c j"), func=ACT.Square
            )
            nc.vector.tensor_tensor(
                out=a_grouped[:, HALF:TOKENS, :],
                in0=relu[:, :, HALF:TOKENS].rearrange("p j c -> p c j"),
                in1=relu[:, :, HALF:TOKENS].rearrange("p j c -> p c j"),
                op=ALU.mult,
            )
            nc.vector.quantize_mx(
                out=a_codes[:].bitcast(FP8X4), scales=a_plane[:], in_=a_grouped[:].rearrange("p c j -> p (c j)")
            )

        acc = keep.tile([P, TOKEN_TILES, D_DIM], F32)
        bod_bc = keep.tile([P, D_DIM], BF16)

        psum = stack.enter_context(tc.psum_pool(name="psum", bufs=2))

        def sums_matmuls(k):
            n, h = k // 2, k % 2
            cols = slice(h * HALF, (h + 1) * HALF)
            if h == 0:
                sums[n] = ring3.tile([P, 2, 2, HALF, 2], F32, name="sums%d" % n, tag="sums")
            for w in range(2):
                vl_ps = psum.tile([P, 2, HALF], F32, name="vl_ps", tag="vl")
                for e in range(2):
                    nc.tensor.matmul(
                        vl_ps[:, e, :],
                        lhsT=kv_sb[:, n * K_PASS + 2 * w + e : (n + 1) * K_PASS : PACK],
                        rhs=qlT[:].rearrange("s t p -> s (t p)")[:, cols],
                        start=True,
                        stop=True,
                    )
                nc.scalar.copy(out=sums[n][:, h, w], in_=vl_ps[:].rearrange("p e c -> p c e"))
                vq_banks[(k, w)] = psum.tile([P, 2, HALF], F32, name="vq_ps", tag="vq")
                for e in range(2):
                    t = 2 * w + e
                    nc.tensor.matmul_mx(
                        out=vq_banks[(k, w)][:, e, :],
                        lhsT=v_codes[n][:, t * P : (t + 1) * P].bitcast(FP8X4),
                        lhsT_scale=v_plane[n][:, t * P : (t + 1) * P],
                        rhs=a_codes[:, cols].bitcast(FP8X4),
                        rhs_scale=a_plane[:, cols],
                        start=True,
                        stop=True,
                    )
                if n + 2 < GROUPS:
                    regroup(nc.scalar.copy, n + 2, 2 * h + w, 2 * h + w + 1)

        def add_sums(k):
            n, h = k // 2, k % 2
            for w in range(2):
                nc.vector.tensor_tensor(
                    out=sums[n][:, h, w],
                    in0=vq_banks[(k, w)][:].rearrange("p e c -> p c e"),
                    in1=sums[n][:, h, w],
                    op=ALU.add,
                )

        def transpose_gate(k):
            n, h = k // 2, k % 2
            c, lo = n // CHUNK_GROUPS, (n % CHUNK_GROUPS) * K_PASS
            gate_banks[k] = psum.tile([P, 2, HALF], F32, name="gate_ps", tag="gate")
            for tile_in_half in range(2):
                words = u_raw[c][:, 2 * h + tile_in_half, lo : lo + K_PASS].bitcast(F32)
                for pair in range(2):
                    nc.tensor.transpose(
                        gate_banks[k][:, pair, tile_in_half * P : (tile_in_half + 1) * P],
                        words[:, pair : K_PASS // 2 : 2],
                        ident_f32[:],
                    )

        def gate(k):
            n, h = k // 2, k % 2
            if h == 0:
                h_grouped[n] = ring2.tile([P, TOKENS, PACK], BF16, name="h_grouped%d" % n, tag="h_grouped", align_bytes=64)
            cols = slice(h * HALF, (h + 1) * HALF)
            nc.vector.tensor_tensor(
                out=h_grouped[n][:, cols, :].rearrange("p c (w e) -> p c w e", w=2),
                in0=sums[n][:, h].rearrange("p w c e -> p c w e"),
                in1=gate_banks[k][:].bitcast(BF16).rearrange("p w (c e) -> p c w e", e=2),
                op=ALU.mult,
            )

        def quantise_h(n):
            r, g = n // ROUND, n % ROUND
            if g == 0:
                h_codes[r] = ring2.tile([P, ROUND, TOKENS], U32, name="h_codes%d" % r, tag="h_codes", align_bytes=64)
                h_plane[r] = ring2.tile([P, ROUND, TOKENS], U8, name="h_plane%d" % r, tag="h_plane", align_bytes=64)
            nc.vector.quantize_mx(
                out=h_codes[r][:, g, :].bitcast(FP8X4),
                scales=h_plane[r][:, g, :],
                in_=h_grouped[n][:].rearrange("p c t -> p (c t)"),
            )

        def project(index):
            r, tile_and_part = index // (2 * TOKEN_TILES), index % (2 * TOKEN_TILES)
            t, part = tile_and_part // 2, tile_and_part % 2
            first, width = D_PARTS[part]
            bank = LAST_ROUND_BANKS[tile_and_part % len(LAST_ROUND_BANKS)] if r == ROUNDS - 1 else "proj"
            proj_ps = psum.tile([P, 512], F32, name="proj_ps", tag=bank)
            for g in range(ROUND):
                nc.tensor.matmul_mx(
                    out=proj_ps[:, 0:width],
                    lhsT=h_codes[r][:, g, t * P : (t + 1) * P].bitcast(FP8X4),
                    lhsT_scale=h_plane[r][:, g, t * P : (t + 1) * P],
                    rhs=w_words[r][:, g, first : first + width].bitcast(FP8X4),
                    rhs_scale=w_planes[:, r * ROUND + g, first : first + width],
                    start=(g == 0),
                    stop=(g == ROUND - 1),
                )
            target = acc[:, t, first : first + width]
            if r < ROUNDS - 1:
                partial = ring2.tile([P, 512], F32, name="partial", tag="partial")
                nc.scalar.copy(out=partial[:, 0:width], in_=proj_ps[:, 0:width])
                so_far = bod_bc[:, first : first + width] if r == 0 else target
                nc.gpsimd.tensor_tensor(out=target, in0=so_far, in1=partial[:, 0:width], op=ALU.add)
            else:
                nc.vector.tensor_tensor(out=target, in0=proj_ps[:, 0:width], in1=target, op=ALU.add)
                if part == 1:
                    nc.sync.dma_start(out=out_rows[:, t, :], in_=acc[:, t, :])

        for k in range(-1, ROUNDS * 2 * TOKEN_TILES + PROJECT_LAG):
            n, h = k // 2, k % 2
            if h == 0 and 0 <= n < GROUPS:
                if n % 2 == 0 and n // 2 + 2 < CHUNKS:
                    load_v(n // 2 + 2)
                    load_u(n // 2 + 2)
                if n % ROUND == 0 and n // ROUND + 1 < ROUNDS:
                    load_kv(n // ROUND + 1)
                if n % ROUND == 2:
                    load_w_words(n // ROUND)
                if n == 1:
                    load_w_scales()
                    nc.sync.dma_start(out=bod_bc[:], in_=bod.partition_broadcast(P))
            if 0 <= k - 2 < HALF_STEPS:
                gate(k - 2)
            if 0 <= k + 1 < HALF_STEPS:
                sums_matmuls(k + 1)
            if 0 <= k < HALF_STEPS:
                add_sums(k)
            if 0 <= k - PROJECT_LAG:
                project(k - PROJECT_LAG)
            if 0 <= k < HALF_STEPS:
                transpose_gate(k)
            if h == 0 and 0 <= n and n + 1 < GROUPS:
                quantise_v(n + 1)
            if h == 1 and 0 <= n - 1 < GROUPS:
                quantise_h(n - 1)
